import numpy as np
import ml_dtypes


def mxq(x, axis, fmt="e4m3"):
    dtype, down = {"e4m3": (ml_dtypes.float8_e4m3fn, 7), "e5m2": (ml_dtypes.float8_e5m2, 14)}[fmt]
    v = np.moveaxis(np.asarray(x, np.float32).astype(ml_dtypes.bfloat16).astype(np.float64), axis, -1)
    blocks = v.reshape(v.shape[:-1] + (-1, 32))
    amax = np.abs(blocks).max(-1, keepdims=True)
    byte = np.maximum(np.where(amax > 0, np.frexp(amax)[1] - 1 + 127, 0) - down, 1)
    scale = np.exp2(byte - 127.0)
    codes = (blocks / scale).astype(np.float32).astype(dtype).astype(np.float64)
    return np.moveaxis((codes * scale).reshape(v.shape), -1, axis)


WIDE = False


def mx_kscale(k):
    if not WIDE:
        return np.ones(k)
    levels = np.array([10, -10, 5, -5, 0])
    a = np.random.permutation(np.resize(levels, k // 512 * 4)).reshape(k // 512, 4)
    idx = np.arange(k)
    return np.exp2(a[idx // 512, idx % 128 // 32])


BF16 = ml_dtypes.bfloat16


def bf(x):
    return np.asarray(x, np.float32).astype(BF16)


def f64(x):
    return np.asarray(x).astype(np.float64)


B, T, D, NH, HD, G, RD, F = 1, 640, 1024, 8, 128, 2, 16, 4096
HKV = NH // G
C = NH * HD


def setup_inputs():
    s = mx_kscale(C).reshape(NH, HD)
    sh = np.where(np.arange(NH) % 2 == 0, s.max(axis=1), s.min(axis=1))
    v = np.random.standard_normal((B, HKV, T, HD))
    a = 0.4 * np.random.standard_normal((B, HKV, G, T, HD)) + 0.4 * v[:, :, None]
    return {"attn_out": bf(a * sh.reshape(HKV, G)[None, :, :, None, None]),
            "v": bf(v),
            "x": bf(np.random.standard_normal((B, T, D)) * np.random.uniform(0.5, 2.0, (B, T, 1))),
            "wo": bf(np.random.standard_normal((D, C)) / np.sqrt(C) / np.repeat(sh, HD)[None, :]),
            "attn_scale": bf(1.0 + 0.1 * np.random.standard_normal(D))}


def reference(attn_out, v, x, wo, attn_scale):
    y_g = f64(attn_out).transpose(0, 3, 1, 2, 4)
    v_t = f64(v).transpose(0, 2, 1, 3)
    vn = v_t / np.maximum(np.sqrt(np.sum(np.square(v_t), axis=-1, keepdims=True)), 1e-12)
    vn = vn[:, :, :, None, :]
    proj = np.sum(y_g * vn, axis=-1, keepdims=True) * vn
    y = (y_g - proj).reshape(B, T, C)
    return f64(x) + f64(attn_scale) * (mxq(y, 2, "e4m3") @ mxq(f64(wo), 1, "e4m3").T)

@@ -1,0 +1,177 @@
+from contextlib import ExitStack
+
+import concourse.mybir as mybir
+from concourse.masks import make_identity
+
+F32 = mybir.dt.float32
+BF16 = mybir.dt.bfloat16
+U32 = mybir.dt.uint32
+U8 = mybir.dt.uint8
+FP8X4 = mybir.dt.float8_e4m3fn_x4
+ALU = mybir.AluOpType
+ACT = mybir.ActivationFunctionType
+
+P = 128
+T = 640
+HKV = 4
+G = 2
+HD = 128
+C = HKV * G * HD
+D = 1024
+
+T_TILES = T // P
+PASSES = C // (4 * P)
+D_HALF = 512
+D_HALVES = D // D_HALF
+ROWS_PER_HALF = D_HALF // P
+
+EPS_SQUARED = 1e-24
+
+FLOPS = 2 * T * C * D
+
+
+def tile_block_pb_kernel(tc, attn_out, v, x, wo, attn_scale, out):
+    nc = tc.nc
+    with ExitStack() as ctx:
+        const = ctx.enter_context(tc.tile_pool(name="const", bufs=1))
+        weights = ctx.enter_context(tc.tile_pool(name="weights", bufs=D_HALVES))
+        tokens = ctx.enter_context(tc.tile_pool(name="tokens", bufs=T_TILES))
+        work = ctx.enter_context(tc.tile_pool(name="work", bufs=3))
+        psum_wo = ctx.enter_context(tc.psum_pool(name="psum_wo", bufs=2))
+        psum_y = ctx.enter_context(tc.psum_pool(name="psum_y", bufs=2))
+        psum_acc = ctx.enter_context(tc.psum_pool(name="psum_acc", bufs=4))
+
+        a_tiles, v_tiles, x_tiles, wo_rows = [], [], [], []
+        for i in range(T_TILES):
+            rows = slice(i * P, (i + 1) * P)
+            v_sb = tokens.tile([P, HKV, HD], BF16)
+            nc.sync.dma_start(out=v_sb[:], in_=v[0, :, rows, :].rearrange("h t d -> t h d"))
+            a_sb = tokens.tile([P, HKV, G, HD], BF16)
+            nc.sync.dma_start(
+                out=a_sb[:], in_=attn_out[0, :, :, rows, :].rearrange("h g t d -> t h g d")
+            )
+            v_tiles.append(v_sb)
+            a_tiles.append(a_sb)
+            half = i - 1
+            if half in range(D_HALVES):
+                wo_sb = weights.tile([P, ROWS_PER_HALF, C], BF16)
+                nc.sync.dma_start(
+                    out=wo_sb[:],
+                    in_=wo[half * D_HALF : (half + 1) * D_HALF, :].rearrange(
+                        "(n p) c -> p n c", p=P
+                    ),
+                )
+                wo_rows.append(wo_sb)
+        gain = const.tile([P, D], BF16)
+        nc.sync.dma_start(out=gain[:], in_=attn_scale.partition_broadcast(P))
+        for i in range(T_TILES):
+            x_sb = tokens.tile([P, D], BF16)
+            nc.sync.dma_start(out=x_sb[:], in_=x[0, i * P : (i + 1) * P, :])
+            x_tiles.append(x_sb)
+
+        ident_f32 = const.tile([P, P], F32)
+        make_identity(nc, ident_f32[:])
+        ident_bf16 = const.tile([P, P], BF16)
+        make_identity(nc, ident_bf16[:])
+
+        wo_codes, wo_scales = [], []
+        for half in range(D_HALVES):
+            grouped = weights.tile([P, PASSES, D_HALF, 2], F32, align_bytes=64, name="wo_grouped")
+            for n in range(ROWS_PER_HALF):
+                words = wo_rows[half][:, n, :].bitcast(F32)
+                wo_t = psum_wo.tile([P, PASSES * 2, P], F32)
+                for j in range(PASSES * 2):
+                    nc.tensor.transpose(
+                        out=wo_t[:, j, :], in_=words[:, j * P : (j + 1) * P], identity=ident_f32[:]
+                    )
+                nc.scalar.copy(
+                    out=grouped[:, :, n * P : (n + 1) * P, :],
+                    in_=wo_t[:].rearrange("p (s u) d -> p s d u", u=2),
+                )
+            codes = weights.tile([P, PASSES, D_HALF], U32, align_bytes=64, name="wo_codes")
+            scales = weights.tile([P, PASSES, D_HALF], U8, align_bytes=64, name="wo_scales")
+            nc.vector.quantize_mx(
+                out=codes[:].rearrange("p s d -> p (s d)").bitcast(FP8X4),
+                scales=scales[:].rearrange("p s d -> p (s d)"),
+                in_=grouped[:].rearrange("p s d u -> p (s d u)").bitcast(BF16),
+            )
+            wo_codes.append(codes)
+            wo_scales.append(scales)
+
+        for i in range(T_TILES):
+            a_sb, v_sb, x_sb = a_tiles[i], v_tiles[i], x_tiles[i]
+
+            scratch = work.tile([P, HD], BF16)
+            v_dot_v = work.tile([P, HKV], F32)
+            for h in range(HKV):
+                nc.scalar.activation(
+                    out=scratch[:], in_=v_sb[:, h, :], func=ACT.Square,
+                    accum_out=v_dot_v[:, h : h + 1],
+                )
+            products = work.tile([P, HKV, G, HD], F32)
+            nc.vector.tensor_tensor(
+                out=products[:], in0=a_sb[:],
+                in1=v_sb[:].unsqueeze(2).to_broadcast([P, HKV, G, HD]), op=ALU.mult,
+            )
+            a_dot_v = work.tile([P, HKV, G], F32)
+            for h in range(HKV):
+                for g in range(G):
+                    nc.scalar.activation(
+                        out=scratch[:], in_=products[:, h, g, :], func=ACT.Copy,
+                        accum_out=a_dot_v[:, h, g : g + 1],
+                    )
+            neg_inv = work.tile([P, HKV], F32)
+            nc.vector.tensor_scalar(
+                out=neg_inv[:], in0=v_dot_v[:], scalar1=EPS_SQUARED, scalar2=-1.0,
+                op0=ALU.max, op1=ALU.mult,
+            )
+            nc.vector.reciprocal(out=neg_inv[:], in_=neg_inv[:])
+            neg_coef = work.tile([P, HKV, G], F32)
+            nc.vector.tensor_tensor(
+                out=neg_coef[:], in0=a_dot_v[:],
+                in1=neg_inv[:].unsqueeze(2).to_broadcast([P, HKV, G]), op=ALU.mult,
+            )
+            y_planes = work.tile([P, HKV, 2, P], BF16)
+            for h in range(HKV):
+                for g in range(G):
+                    nc.vector.scalar_tensor_tensor(
+                        out=y_planes[:, h, :, g * (HD // 2) : (g + 1) * (HD // 2)],
+                        in0=v_sb[:, h, :].rearrange("p (q e) -> p e q", e=2),
+                        scalar=neg_coef[:, h, g : g + 1],
+                        in1=a_sb[:, h, g, :].rearrange("p (q e) -> p e q", e=2),
+                        op0=ALU.mult, op1=ALU.add,
+                    )
+
+            y_t = psum_y.tile([P, HKV * 2, P], BF16)
+            for plane in range(HKV * 2):
+                nc.tensor.transpose(
+                    out=y_t[:, plane, :], in_=y_planes[:, plane // 2, plane % 2, :],
+                    identity=ident_bf16[:],
+                )
+            y_grouped = work.tile([P, PASSES, P, 4], BF16, align_bytes=64)
+            nc.scalar.copy(out=y_grouped[:], in_=y_t[:].rearrange("p (s j) t -> p s t j", j=4))
+            y_codes = work.tile([P, PASSES, P], U32, align_bytes=64)
+            y_scales = work.tile([P, PASSES, P], U8, align_bytes=64)
+            nc.vector.quantize_mx(
+                out=y_codes[:].rearrange("p s t -> p (s t)").bitcast(FP8X4),
+                scales=y_scales[:].rearrange("p s t -> p (s t)"),
+                in_=y_grouped[:].rearrange("p s t j -> p (s t j)"),
+            )
+
+            for half in range(D_HALVES):
+                cols = slice(half * D_HALF, (half + 1) * D_HALF)
+                acc = psum_acc.tile([P, D_HALF], F32)
+                for s in range(PASSES):
+                    nc.tensor.matmul_mx(
+                        out=acc[:],
+                        lhsT=y_codes[:, s, :].bitcast(FP8X4),
+                        lhsT_scale=y_scales[:, s, :],
+                        rhs=wo_codes[half][:, s, :].bitcast(FP8X4),
+                        rhs_scale=wo_scales[half][:, s, :],
+                        start=(s == 0),
+                        stop=(s == PASSES - 1),
+                    )
+                result = work.tile([P, D_HALF], F32)
+                nc.vector.tensor_tensor(out=result[:], in0=acc[:], in1=gain[:, cols], op=ALU.mult)
+                nc.vector.tensor_tensor(out=result[:], in0=result[:], in1=x_sb[:, cols], op=ALU.add)
+                nc.sync.dma_start(out=out[0, i * P : (i + 1) * P, cols], in_=result[:])

@@ -23,7 +23,7 @@ T_TILES = T // P
 PASSES = C // (4 * P)
 D_HALF = 512
 D_HALVES = D // D_HALF
-ROWS_PER_HALF = D_HALF // P
+D_BLOCKS = D_HALF // P
 
 EPS_SQUARED = 1e-24
 
@@ -37,11 +37,16 @@ def tile_block_pb_kernel(tc, attn_out, v, x, wo, attn_scale, out):
         weights = ctx.enter_context(tc.tile_pool(name="weights", bufs=D_HALVES))
         tokens = ctx.enter_context(tc.tile_pool(name="tokens", bufs=T_TILES))
         work = ctx.enter_context(tc.tile_pool(name="work", bufs=3))
-        psum_wo = ctx.enter_context(tc.psum_pool(name="psum_wo", bufs=2))
-        psum_y = ctx.enter_context(tc.psum_pool(name="psum_y", bufs=2))
-        psum_acc = ctx.enter_context(tc.psum_pool(name="psum_acc", bufs=4))
+        psum_in = ctx.enter_context(tc.psum_pool(name="psum_in", bufs=3))
+        psum_acc = ctx.enter_context(tc.psum_pool(name="psum_acc", bufs=3))
+        psum_back = ctx.enter_context(tc.psum_pool(name="psum_back", bufs=2))
 
         a_tiles, v_tiles, x_tiles, wo_rows = [], [], [], []
+        gain_rows = const.tile([P, P], BF16)
+        nc.gpsimd.memset(gain_rows[:], 0.0)
+        nc.scalar.dma_start(
+            out=gain_rows[0 : D // P, :], in_=attn_scale.rearrange("(n p) -> n p", p=P)
+        )
         for i in range(T_TILES):
             rows = slice(i * P, (i + 1) * P)
             v_sb = tokens.tile([P, HKV, HD], BF16)
@@ -54,7 +59,7 @@ def tile_block_pb_kernel(tc, attn_out, v, x, wo, attn_scale, out):
             a_tiles.append(a_sb)
             half = i - 1
             if half in range(D_HALVES):
-                wo_sb = weights.tile([P, ROWS_PER_HALF, C], BF16)
+                wo_sb = weights.tile([P, D_BLOCKS, C], BF16)
                 nc.sync.dma_start(
                     out=wo_sb[:],
                     in_=wo[half * D_HALF : (half + 1) * D_HALF, :].rearrange(
@@ -62,8 +67,6 @@ def tile_block_pb_kernel(tc, attn_out, v, x, wo, attn_scale, out):
                     ),
                 )
                 wo_rows.append(wo_sb)
-        gain = const.tile([P, D], BF16)
-        nc.sync.dma_start(out=gain[:], in_=attn_scale.partition_broadcast(P))
         for i in range(T_TILES):
             x_sb = tokens.tile([P, D], BF16)
             nc.sync.dma_start(out=x_sb[:], in_=x[0, i * P : (i + 1) * P, :])
@@ -74,104 +77,196 @@ def tile_block_pb_kernel(tc, attn_out, v, x, wo, attn_scale, out):
         ident_bf16 = const.tile([P, P], BF16)
         make_identity(nc, ident_bf16[:])
 
-        wo_codes, wo_scales = [], []
-        for half in range(D_HALVES):
-            grouped = weights.tile([P, PASSES, D_HALF, 2], F32, align_bytes=64, name="wo_grouped")
-            for n in range(ROWS_PER_HALF):
-                words = wo_rows[half][:, n, :].bitcast(F32)
-                wo_t = psum_wo.tile([P, PASSES * 2, P], F32)
-                for j in range(PASSES * 2):
-                    nc.tensor.transpose(
-                        out=wo_t[:, j, :], in_=words[:, j * P : (j + 1) * P], identity=ident_f32[:]
-                    )
-                nc.scalar.copy(
-                    out=grouped[:, :, n * P : (n + 1) * P, :],
-                    in_=wo_t[:].rearrange("p (s u) d -> p s d u", u=2),
-                )
-            codes = weights.tile([P, PASSES, D_HALF], U32, align_bytes=64, name="wo_codes")
-            scales = weights.tile([P, PASSES, D_HALF], U8, align_bytes=64, name="wo_scales")
-            nc.vector.quantize_mx(
-                out=codes[:].rearrange("p s d -> p (s d)").bitcast(FP8X4),
-                scales=scales[:].rearrange("p s d -> p (s d)"),
-                in_=grouped[:].rearrange("p s d u -> p (s d u)").bitcast(BF16),
-            )
-            wo_codes.append(codes)
-            wo_scales.append(scales)
+        products, v_dot_v, neg_inv, neg_coef = {}, {}, {}, {}
+        y_rows, y_grouped, y_codes, y_scales = {}, {}, {}, {}
+        wo_grouped, wo_codes, wo_scales = {}, {}, {}
+        scaled = {}
 
-        for i in range(T_TILES):
-            a_sb, v_sb, x_sb = a_tiles[i], v_tiles[i], x_tiles[i]
-
-            scratch = work.tile([P, HD], BF16)
-            v_dot_v = work.tile([P, HKV], F32)
+        def squares(i):
+            v_dot_v[i] = tokens.tile([P, HKV], F32, name="v_dot_v")
             for h in range(HKV):
+                scratch = work.tile([P, HD], BF16, name="scratch")
                 nc.scalar.activation(
-                    out=scratch[:], in_=v_sb[:, h, :], func=ACT.Square,
-                    accum_out=v_dot_v[:, h : h + 1],
+                    out=scratch[:], in_=v_tiles[i][:, h, :], func=ACT.Square,
+                    accum_out=v_dot_v[i][:, h : h + 1],
                 )
-            products = work.tile([P, HKV, G, HD], F32)
+
+        def multiply(i):
+            products[i] = work.tile([P, HKV, G, HD], F32, name="products")
             nc.vector.tensor_tensor(
-                out=products[:], in0=a_sb[:],
-                in1=v_sb[:].unsqueeze(2).to_broadcast([P, HKV, G, HD]), op=ALU.mult,
+                out=products[i][:], in0=a_tiles[i][:],
+                in1=v_tiles[i][:].unsqueeze(2).to_broadcast([P, HKV, G, HD]), op=ALU.mult,
             )
-            a_dot_v = work.tile([P, HKV, G], F32)
-            for h in range(HKV):
-                for g in range(G):
-                    nc.scalar.activation(
-                        out=scratch[:], in_=products[:, h, g, :], func=ACT.Copy,
-                        accum_out=a_dot_v[:, h, g : g + 1],
-                    )
-            neg_inv = work.tile([P, HKV], F32)
+
+        def invert(i):
+            neg_norm = tokens.tile([P, HKV], F32, name="neg_norm")
             nc.vector.tensor_scalar(
-                out=neg_inv[:], in0=v_dot_v[:], scalar1=EPS_SQUARED, scalar2=-1.0,
+                out=neg_norm[:], in0=v_dot_v[i][:], scalar1=EPS_SQUARED, scalar2=-1.0,
                 op0=ALU.max, op1=ALU.mult,
             )
-            nc.vector.reciprocal(out=neg_inv[:], in_=neg_inv[:])
-            neg_coef = work.tile([P, HKV, G], F32)
-            nc.vector.tensor_tensor(
-                out=neg_coef[:], in0=a_dot_v[:],
-                in1=neg_inv[:].unsqueeze(2).to_broadcast([P, HKV, G]), op=ALU.mult,
-            )
-            y_planes = work.tile([P, HKV, 2, P], BF16)
+            neg_inv[i] = tokens.tile([P, HKV], F32, name="neg_inv")
+            nc.vector.reciprocal(out=neg_inv[i][:], in_=neg_norm[:])
+
+        def sums(i):
+            neg_coef[i] = tokens.tile([P, HKV, G], F32, name="neg_coef")
+            for h in range(HKV):
+                for g in range(G):
+                    scratch = work.tile([P, HD], BF16, name="scratch")
+                    nc.scalar.activation(
+                        out=scratch[:], in_=products[i][:, h, g, :], func=ACT.Copy,
+                        scale=neg_inv[i][:, h : h + 1], accum_out=neg_coef[i][:, h, g : g + 1],
+                    )
+
+        def subtract(i):
+            y_rows[i] = work.tile([P, HKV, G, HD], BF16, align_bytes=64, name="y_rows")
             for h in range(HKV):
                 for g in range(G):
                     nc.vector.scalar_tensor_tensor(
-                        out=y_planes[:, h, :, g * (HD // 2) : (g + 1) * (HD // 2)],
-                        in0=v_sb[:, h, :].rearrange("p (q e) -> p e q", e=2),
-                        scalar=neg_coef[:, h, g : g + 1],
-                        in1=a_sb[:, h, g, :].rearrange("p (q e) -> p e q", e=2),
+                        out=y_rows[i][:, h, g, :], in0=v_tiles[i][:, h, :],
+                        scalar=neg_coef[i][:, h, g : g + 1], in1=a_tiles[i][:, h, g, :],
                         op0=ALU.mult, op1=ALU.add,
                     )
 
-            y_t = psum_y.tile([P, HKV * 2, P], BF16)
-            for plane in range(HKV * 2):
+        def words_to_partitions(rows, grouped):
+            words = rows.bitcast(F32)
+            turned = psum_in.tile([P, PASSES * 2, P], F32, name="turned")
+            for j in range(PASSES * 2):
                 nc.tensor.transpose(
-                    out=y_t[:, plane, :], in_=y_planes[:, plane // 2, plane % 2, :],
-                    identity=ident_bf16[:],
+                    out=turned[:, j, :], in_=words[:, j * P : (j + 1) * P], identity=ident_f32[:]
                 )
-            y_grouped = work.tile([P, PASSES, P, 4], BF16, align_bytes=64)
-            nc.scalar.copy(out=y_grouped[:], in_=y_t[:].rearrange("p (s j) t -> p s t j", j=4))
-            y_codes = work.tile([P, PASSES, P], U32, align_bytes=64)
-            y_scales = work.tile([P, PASSES, P], U8, align_bytes=64)
+            nc.scalar.copy(out=grouped, in_=turned[:].rearrange("p (s u) r -> p s r u", u=2))
+
+        def y_turn(i):
+            y_grouped[i] = work.tile([P, PASSES, P, 2], F32, align_bytes=64, name="y_grouped")
+            words_to_partitions(y_rows[i][:].rearrange("p h g d -> p (h g d)"), y_grouped[i][:])
+
+        def y_quantise(i):
+            y_codes[i] = tokens.tile([P, PASSES, P], U32, align_bytes=64, name="y_codes")
+            y_scales[i] = tokens.tile([P, PASSES, P], U8, align_bytes=64, name="y_scales")
             nc.vector.quantize_mx(
-                out=y_codes[:].rearrange("p s t -> p (s t)").bitcast(FP8X4),
-                scales=y_scales[:].rearrange("p s t -> p (s t)"),
-                in_=y_grouped[:].rearrange("p s t j -> p (s t j)"),
+                out=y_codes[i][:].rearrange("p s t -> p (s t)").bitcast(FP8X4),
+                scales=y_scales[i][:].rearrange("p s t -> p (s t)"),
+                in_=y_grouped[i][:].rearrange("p s t u -> p (s t u)").bitcast(BF16),
             )
 
-            for half in range(D_HALVES):
-                cols = slice(half * D_HALF, (half + 1) * D_HALF)
-                acc = psum_acc.tile([P, D_HALF], F32)
+        def wo_turn(half, n):
+            if half not in wo_grouped:
+                wo_grouped[half] = weights.tile(
+                    [P, PASSES, D_HALF, 2], F32, align_bytes=64, name="wo_grouped"
+                )
+            words_to_partitions(
+                wo_rows[half][:, n, :], wo_grouped[half][:, :, n * P : (n + 1) * P, :]
+            )
+
+        def wo_quantise(half):
+            wo_codes[half] = weights.tile([P, PASSES, D_HALF], U32, align_bytes=64, name="wo_codes")
+            wo_scales[half] = weights.tile([P, PASSES, D_HALF], U8, align_bytes=64, name="wo_scales")
+            nc.vector.quantize_mx(
+                out=wo_codes[half][:].rearrange("p s d -> p (s d)").bitcast(FP8X4),
+                scales=wo_scales[half][:].rearrange("p s d -> p (s d)"),
+                in_=wo_grouped[half][:].rearrange("p s d u -> p (s d u)").bitcast(BF16),
+            )
+
+        def project(i, half):
+            acc = psum_acc.tile([P, D_BLOCKS, P], F32, name="acc")
+            for n in range(D_BLOCKS):
                 for s in range(PASSES):
                     nc.tensor.matmul_mx(
-                        out=acc[:],
-                        lhsT=y_codes[:, s, :].bitcast(FP8X4),
-                        lhsT_scale=y_scales[:, s, :],
-                        rhs=wo_codes[half][:, s, :].bitcast(FP8X4),
-                        rhs_scale=wo_scales[half][:, s, :],
+                        out=acc[:, n, :],
+                        lhsT=wo_codes[half][:, s, n * P : (n + 1) * P].bitcast(FP8X4),
+                        lhsT_scale=wo_scales[half][:, s, n * P : (n + 1) * P],
+                        rhs=y_codes[i][:, s, :].bitcast(FP8X4),
+                        rhs_scale=y_scales[i][:, s, :],
                         start=(s == 0),
                         stop=(s == PASSES - 1),
                     )
-                result = work.tile([P, D_HALF], F32)
-                nc.vector.tensor_tensor(out=result[:], in0=acc[:], in1=gain[:, cols], op=ALU.mult)
-                nc.vector.tensor_tensor(out=result[:], in0=result[:], in1=x_sb[:, cols], op=ALU.add)
-                nc.sync.dma_start(out=out[0, i * P : (i + 1) * P, cols], in_=result[:])
+            scaled[i, half] = work.tile([P, D_BLOCKS, P], F32, name="scaled", bufs=4)
+            for n in range(D_BLOCKS):
+                block = half * D_BLOCKS + n
+                nc.scalar.activation(
+                    out=scaled[i, half][:, n, :], in_=acc[:, n, :], func=ACT.Copy,
+                    scale=gain[:, block : block + 1],
+                )
+
+        def finish(i, half):
+            cols = slice(half * D_HALF, (half + 1) * D_HALF)
+            back = psum_back.tile([P, D_BLOCKS, P], F32, name="back")
+            for n in range(D_BLOCKS):
+                nc.tensor.transpose(
+                    out=back[:, n, :], in_=scaled[i, half][:, n, :], identity=ident_f32[:]
+                )
+            result = work.tile([P, D_HALF], F32, name="result", bufs=4)
+            nc.vector.tensor_tensor(
+                out=result[:], in0=back[:].rearrange("p n d -> p (n d)"), in1=x_tiles[i][:, cols],
+                op=ALU.add,
+            )
+            nc.sync.dma_start(out=out[0, i * P : (i + 1) * P, cols], in_=result[:])
+
+        ctx.enter_context(tc.manual_schedule())
+        squares(0)
+        multiply(0)
+        invert(0)
+        squares(1)
+        multiply(1)
+        sums(0)
+        invert(1)
+        subtract(0)
+        sums(1)
+        gain_turned = psum_in.tile([P, P], BF16, name="turned")
+        nc.tensor.transpose(out=gain_turned[:], in_=gain_rows[:], identity=ident_bf16[:])
+        gain = const.tile([P, D // P], F32)
+        nc.scalar.copy(out=gain[:], in_=gain_turned[:, 0 : D // P])
+        wo_turn(0, 0)
+        wo_turn(0, 1)
+        y_turn(0)
+        multiply(2)
+        wo_turn(0, 2)
+        wo_turn(0, 3)
+        subtract(1)
+        squares(2)
+        y_turn(1)
+        y_quantise(0)
+        invert(2)
+        sums(2)
+        wo_quantise(0)
+        multiply(3)
+        y_quantise(1)
+        for n in range(D_BLOCKS):
+            wo_turn(1, n)
+        subtract(2)
+        squares(3)
+        y_turn(2)
+        wo_quantise(1)
+        invert(3)
+        sums(3)
+        multiply(4)
+        y_quantise(2)
+        project(0, 0)
+        project(0, 1)
+        subtract(3)
+        squares(4)
+        y_turn(3)
+        finish(0, 0)
+        finish(0, 1)
+        invert(4)
+        sums(4)
+        y_quantise(3)
+        project(1, 0)
+        project(1, 1)
+        subtract(4)
+        y_turn(4)
+        finish(1, 0)
+        finish(1, 1)
+        project(2, 0)
+        y_quantise(4)
+        project(2, 1)
+        project(3, 0)
+        finish(2, 0)
+        finish(2, 1)
+        project(3, 1)
+        project(4, 0)
+        finish(3, 0)
+        finish(3, 1)
+        project(4, 1)
+        finish(4, 0)
+        finish(4, 1)

@@ -20,6 +20,7 @@ C = HKV * G * HD
 D = 1024
 
 T_TILES = T // P
+GROUPS = (1, 2, 2)
 PASSES = C // (4 * P)
 D_HALF = 512
 D_HALVES = D // D_HALF
@@ -37,27 +38,33 @@ def tile_block_pb_kernel(tc, attn_out, v, x, wo, attn_scale, out):
         weights = ctx.enter_context(tc.tile_pool(name="weights", bufs=D_HALVES))
         tokens = ctx.enter_context(tc.tile_pool(name="tokens", bufs=T_TILES))
         work = ctx.enter_context(tc.tile_pool(name="work", bufs=3))
-        psum_in = ctx.enter_context(tc.psum_pool(name="psum_in", bufs=3))
-        psum_acc = ctx.enter_context(tc.psum_pool(name="psum_acc", bufs=3))
-        psum_back = ctx.enter_context(tc.psum_pool(name="psum_back", bufs=2))
+        psum = ctx.enter_context(tc.psum_pool(name="psum", bufs=8))
 
-        a_tiles, v_tiles, x_tiles, wo_rows = [], [], [], []
+        a_tiles, v_tiles, x_tiles, out_rows, groups, wo_rows = [], [], [], [], [], []
         gain_rows = const.tile([P, P], BF16)
         nc.gpsimd.memset(gain_rows[:], 0.0)
         nc.scalar.dma_start(
             out=gain_rows[0 : D // P, :], in_=attn_scale.rearrange("(n p) -> n p", p=P)
         )
-        for i in range(T_TILES):
-            rows = slice(i * P, (i + 1) * P)
-            v_sb = tokens.tile([P, HKV, HD], BF16)
-            nc.sync.dma_start(out=v_sb[:], in_=v[0, :, rows, :].rearrange("h t d -> t h d"))
-            a_sb = tokens.tile([P, HKV, G, HD], BF16)
+        first = 0
+        for k, n in enumerate(GROUPS):
+            rows = slice(first, first + n * P)
+            v_sb = tokens.tile([P, HKV, n, HD], BF16, name="v_sb_%d" % k, bufs=1)
             nc.sync.dma_start(
-                out=a_sb[:], in_=attn_out[0, :, :, rows, :].rearrange("h g t d -> t h g d")
+                out=v_sb[:], in_=v[0, :, rows, :].rearrange("h (p j) d -> p h j d", j=n)
             )
-            v_tiles.append(v_sb)
-            a_tiles.append(a_sb)
-            half = i - 1
+            a_sb = tokens.tile([P, HKV * G, n, HD], BF16, name="a_sb_%d" % k, bufs=1)
+            nc.sync.dma_start(
+                out=a_sb[:],
+                in_=attn_out[0, :, :, rows, :].rearrange("h g (p j) d -> p (h g) j d", j=n),
+            )
+            for j in range(n):
+                v_tiles.append(v_sb[:, :, j, :])
+                a_tiles.append(a_sb[:, :, j, :].rearrange("p (h g) d -> p h g d", g=G))
+                out_rows.append(out[0, rows, :].rearrange("(p j) d -> p j d", j=n)[:, j, :])
+            groups.append((rows, n))
+            first += n * P
+            half = k - 1
             if half in range(D_HALVES):
                 wo_sb = weights.tile([P, D_BLOCKS, C], BF16)
                 nc.sync.dma_start(
@@ -67,10 +74,13 @@ def tile_block_pb_kernel(tc, attn_out, v, x, wo, attn_scale, out):
                     ),
                 )
                 wo_rows.append(wo_sb)
-        for i in range(T_TILES):
-            x_sb = tokens.tile([P, D], BF16)
-            nc.sync.dma_start(out=x_sb[:], in_=x[0, i * P : (i + 1) * P, :])
-            x_tiles.append(x_sb)
+        for k, (rows, n) in enumerate(groups):
+            x_sb = tokens.tile([P, n, D], BF16, name="x_sb_%d" % k, bufs=1)
+            nc.sync.dma_start(
+                out=x_sb[:], in_=x[0, rows, :].rearrange("(p j) d -> p j d", j=n)
+            )
+            for j in range(n):
+                x_tiles.append(x_sb[:, j, :])
 
         ident_f32 = const.tile([P, P], F32)
         make_identity(nc, ident_f32[:])
@@ -80,7 +90,7 @@ def tile_block_pb_kernel(tc, attn_out, v, x, wo, attn_scale, out):
         products, v_dot_v, neg_inv, neg_coef = {}, {}, {}, {}
         y_rows, y_grouped, y_codes, y_scales = {}, {}, {}, {}
         wo_grouped, wo_codes, wo_scales = {}, {}, {}
-        scaled = {}
+        acc, scaled, back = {}, {}, {}
 
         def squares(i):
             v_dot_v[i] = tokens.tile([P, HKV], F32, name="v_dot_v")
@@ -92,10 +102,10 @@ def tile_block_pb_kernel(tc, attn_out, v, x, wo, attn_scale, out):
                 )
 
         def multiply(i):
-            products[i] = work.tile([P, HKV, G, HD], F32, name="products")
+            products[i] = tokens.tile([P, HKV, G, HD], F32, name="products")
             nc.vector.tensor_tensor(
-                out=products[i][:], in0=a_tiles[i][:],
-                in1=v_tiles[i][:].unsqueeze(2).to_broadcast([P, HKV, G, HD]), op=ALU.mult,
+                out=products[i][:], in0=a_tiles[i],
+                in1=v_tiles[i].unsqueeze(2).to_broadcast([P, HKV, G, HD]), op=ALU.mult,
             )
 
         def invert(i):
@@ -129,7 +139,7 @@ def tile_block_pb_kernel(tc, attn_out, v, x, wo, attn_scale, out):
 
         def words_to_partitions(rows, grouped):
             words = rows.bitcast(F32)
-            turned = psum_in.tile([P, PASSES * 2, P], F32, name="turned")
+            turned = psum.tile([P, PASSES * 2, P], F32, name="bank")
             for j in range(PASSES * 2):
                 nc.tensor.transpose(
                     out=turned[:, j, :], in_=words[:, j * P : (j + 1) * P], identity=ident_f32[:]
@@ -168,11 +178,11 @@ def tile_block_pb_kernel(tc, attn_out, v, x, wo, attn_scale, out):
             )
 
         def project(i, half):
-            acc = psum_acc.tile([P, D_BLOCKS, P], F32, name="acc")
+            acc[i, half] = psum.tile([P, D_BLOCKS, P], F32, name="bank")
             for n in range(D_BLOCKS):
                 for s in range(PASSES):
                     nc.tensor.matmul_mx(
-                        out=acc[:, n, :],
+                        out=acc[i, half][:, n, :],
                         lhsT=wo_codes[half][:, s, n * P : (n + 1) * P].bitcast(FP8X4),
                         lhsT_scale=wo_scales[half][:, s, n * P : (n + 1) * P],
                         rhs=y_codes[i][:, s, :].bitcast(FP8X4),
@@ -180,93 +190,100 @@ def tile_block_pb_kernel(tc, attn_out, v, x, wo, attn_scale, out):
                         start=(s == 0),
                         stop=(s == PASSES - 1),
                     )
+
+        def scale(i, half):
             scaled[i, half] = work.tile([P, D_BLOCKS, P], F32, name="scaled", bufs=4)
             for n in range(D_BLOCKS):
                 block = half * D_BLOCKS + n
                 nc.scalar.activation(
-                    out=scaled[i, half][:, n, :], in_=acc[:, n, :], func=ACT.Copy,
+                    out=scaled[i, half][:, n, :], in_=acc[i, half][:, n, :], func=ACT.Copy,
                     scale=gain[:, block : block + 1],
+                )
+
+        def turn_back(i, half):
+            back[i, half] = psum.tile([P, D_BLOCKS, P], F32, name="bank")
+            for n in range(D_BLOCKS):
+                nc.tensor.transpose(
+                    out=back[i, half][:, n, :], in_=scaled[i, half][:, n, :], identity=ident_f32[:]
                 )
 
         def finish(i, half):
             cols = slice(half * D_HALF, (half + 1) * D_HALF)
-            back = psum_back.tile([P, D_BLOCKS, P], F32, name="back")
-            for n in range(D_BLOCKS):
-                nc.tensor.transpose(
-                    out=back[:, n, :], in_=scaled[i, half][:, n, :], identity=ident_f32[:]
-                )
             result = work.tile([P, D_HALF], F32, name="result", bufs=4)
             nc.vector.tensor_tensor(
-                out=result[:], in0=back[:].rearrange("p n d -> p (n d)"), in1=x_tiles[i][:, cols],
-                op=ALU.add,
+                out=result[:], in0=back[i, half][:].rearrange("p n d -> p (n d)"),
+                in1=x_tiles[i][:, cols], op=ALU.add,
             )
-            nc.sync.dma_start(out=out[0, i * P : (i + 1) * P, cols], in_=result[:])
+            nc.sync.dma_start(out=out_rows[i][:, cols], in_=result[:])
 
         ctx.enter_context(tc.manual_schedule())
         squares(0)
         multiply(0)
         invert(0)
         squares(1)
+        squares(2)
         multiply(1)
         sums(0)
         invert(1)
-        subtract(0)
+        invert(2)
+        multiply(2)
         sums(1)
-        gain_turned = psum_in.tile([P, P], BF16, name="turned")
+        subtract(0)
+        multiply(3)
+        squares(3)
+        squares(4)
+        invert(3)
+        invert(4)
+        for n in range(D_BLOCKS):
+            wo_turn(0, n)
+        gain_turned = psum.tile([P, P], BF16, name="bank")
         nc.tensor.transpose(out=gain_turned[:], in_=gain_rows[:], identity=ident_bf16[:])
         gain = const.tile([P, D // P], F32)
         nc.scalar.copy(out=gain[:], in_=gain_turned[:, 0 : D // P])
-        wo_turn(0, 0)
-        wo_turn(0, 1)
         y_turn(0)
-        multiply(2)
-        wo_turn(0, 2)
-        wo_turn(0, 3)
         subtract(1)
-        squares(2)
-        y_turn(1)
-        y_quantise(0)
-        invert(2)
-        sums(2)
-        wo_quantise(0)
-        multiply(3)
-        y_quantise(1)
         for n in range(D_BLOCKS):
             wo_turn(1, n)
-        subtract(2)
-        squares(3)
-        y_turn(2)
-        wo_quantise(1)
-        invert(3)
-        sums(3)
+        y_turn(1)
+        y_quantise(0)
+        wo_quantise(0)
         multiply(4)
-        y_quantise(2)
-        project(0, 0)
-        project(0, 1)
+        wo_quantise(1)
+        y_quantise(1)
+        for i in range(2, T_TILES):
+            sums(i)
+        for i in range(2):
+            for half in range(D_HALVES):
+                project(i, half)
+        subtract(2)
+        y_turn(2)
         subtract(3)
-        squares(4)
-        y_turn(3)
-        finish(0, 0)
-        finish(0, 1)
-        invert(4)
-        sums(4)
-        y_quantise(3)
-        project(1, 0)
-        project(1, 1)
+        y_quantise(2)
         subtract(4)
-        y_turn(4)
-        finish(1, 0)
-        finish(1, 1)
+        scale(0, 0)
+        scale(0, 1)
+        y_turn(3)
         project(2, 0)
-        y_quantise(4)
         project(2, 1)
-        project(3, 0)
-        finish(2, 0)
-        finish(2, 1)
-        project(3, 1)
-        project(4, 0)
-        finish(3, 0)
-        finish(3, 1)
-        project(4, 1)
-        finish(4, 0)
-        finish(4, 1)
+        turn_back(0, 0)
+        turn_back(0, 1)
+        finish(0, 0)
+        y_quantise(3)
+        finish(0, 1)
+        scale(1, 0)
+        scale(1, 1)
+        y_turn(4)
+        turn_back(1, 0)
+        turn_back(1, 1)
+        finish(1, 0)
+        y_quantise(4)
+        finish(1, 1)
+        for i in range(2, T_TILES):
+            for half in range(D_HALVES):
+                scale(i, half)
+            if i + 1 < T_TILES:
+                project(i + 1, 0)
+                project(i + 1, 1)
+            for half in range(D_HALVES):
+                turn_back(i, half)
+                finish(i, half)

@@ -40,7 +40,8 @@ def tile_block_pb_kernel(tc, attn_out, v, x, wo, attn_scale, out):
         work = ctx.enter_context(tc.tile_pool(name="work", bufs=3))
         psum = ctx.enter_context(tc.psum_pool(name="psum", bufs=8))
 
-        a_tiles, v_tiles, x_tiles, out_rows, groups, wo_rows = [], [], [], [], [], []
+        a_tiles, v_tiles, x_tiles, out_rows = [], [], [], []
+        groups, group_of, wo_rows = [], [], []
         gain_rows = const.tile([P, P], BF16)
         nc.gpsimd.memset(gain_rows[:], 0.0)
         nc.scalar.dma_start(
@@ -59,6 +60,7 @@ def tile_block_pb_kernel(tc, attn_out, v, x, wo, attn_scale, out):
                 in_=attn_out[0, :, :, rows, :].rearrange("h g (p j) d -> p (h g) j d", j=n),
             )
             for j in range(n):
+                group_of.append((k, j))
                 v_tiles.append(v_sb[:, :, j, :])
                 a_tiles.append(a_sb[:, :, j, :].rearrange("p (h g) d -> p h g d", g=G))
                 out_rows.append(out[0, rows, :].rearrange("(p j) d -> p j d", j=n)[:, j, :])
@@ -82,6 +84,11 @@ def tile_block_pb_kernel(tc, attn_out, v, x, wo, attn_scale, out):
             for j in range(n):
                 x_tiles.append(x_sb[:, j, :])
 
+        gain_free = const.tile([P, D_HALF], BF16)
+        nc.sync.dma_start(
+            out=gain_free[:], in_=attn_scale[0:D_HALF].partition_broadcast(P)
+        )
+
         ident_f32 = const.tile([P, P], F32)
         make_identity(nc, ident_f32[:])
         ident_bf16 = const.tile([P, P], BF16)
@@ -91,14 +98,17 @@ def tile_block_pb_kernel(tc, attn_out, v, x, wo, attn_scale, out):
         y_rows, y_grouped, y_codes, y_scales = {}, {}, {}, {}
         wo_grouped, wo_codes, wo_scales = {}, {}, {}
         acc, scaled, back = {}, {}, {}
+        token_acc, token_scaled = {}, {}
 
         def squares(i):
-            v_dot_v[i] = tokens.tile([P, HKV], F32, name="v_dot_v")
+            k, j = group_of[i]
+            if k not in v_dot_v:
+                v_dot_v[k] = tokens.tile([P, GROUPS[k], HKV], F32, name="v_dot_v")
             for h in range(HKV):
                 scratch = work.tile([P, HD], BF16, name="scratch")
                 nc.scalar.activation(
                     out=scratch[:], in_=v_tiles[i][:, h, :], func=ACT.Square,
-                    accum_out=v_dot_v[i][:, h : h + 1],
+                    accum_out=v_dot_v[k][:, j, h : h + 1],
                 )
 
         def multiply(i):
@@ -108,23 +118,24 @@ def tile_block_pb_kernel(tc, attn_out, v, x, wo, attn_scale, out):
                 in1=v_tiles[i].unsqueeze(2).to_broadcast([P, HKV, G, HD]), op=ALU.mult,
             )
 
-        def invert(i):
-            neg_norm = tokens.tile([P, HKV], F32, name="neg_norm")
+        def invert(k):
+            neg_norm = tokens.tile([P, GROUPS[k], HKV], F32, name="neg_norm")
             nc.vector.tensor_scalar(
-                out=neg_norm[:], in0=v_dot_v[i][:], scalar1=EPS_SQUARED, scalar2=-1.0,
+                out=neg_norm[:], in0=v_dot_v[k][:], scalar1=EPS_SQUARED, scalar2=-1.0,
                 op0=ALU.max, op1=ALU.mult,
             )
-            neg_inv[i] = tokens.tile([P, HKV], F32, name="neg_inv")
-            nc.vector.reciprocal(out=neg_inv[i][:], in_=neg_norm[:])
+            neg_inv[k] = tokens.tile([P, GROUPS[k], HKV], F32, name="neg_inv")
+            nc.vector.reciprocal(out=neg_inv[k][:], in_=neg_norm[:])
 
         def sums(i):
+            k, j = group_of[i]
             neg_coef[i] = tokens.tile([P, HKV, G], F32, name="neg_coef")
             for h in range(HKV):
                 for g in range(G):
                     scratch = work.tile([P, HD], BF16, name="scratch")
                     nc.scalar.activation(
                         out=scratch[:], in_=products[i][:, h, g, :], func=ACT.Copy,
-                        scale=neg_inv[i][:, h : h + 1], accum_out=neg_coef[i][:, h, g : g + 1],
+                        scale=neg_inv[k][:, j, h : h + 1], accum_out=neg_coef[i][:, h, g : g + 1],
                     )
 
         def subtract(i):
@@ -137,14 +148,14 @@ def tile_block_pb_kernel(tc, attn_out, v, x, wo, attn_scale, out):
                         op0=ALU.mult, op1=ALU.add,
                     )
 
-        def words_to_partitions(rows, grouped):
+        def words_to_partitions(rows, grouped, copy=nc.scalar.copy):
             words = rows.bitcast(F32)
             turned = psum.tile([P, PASSES * 2, P], F32, name="bank")
             for j in range(PASSES * 2):
                 nc.tensor.transpose(
                     out=turned[:, j, :], in_=words[:, j * P : (j + 1) * P], identity=ident_f32[:]
                 )
-            nc.scalar.copy(out=grouped, in_=turned[:].rearrange("p (s u) r -> p s r u", u=2))
+            copy(out=grouped, in_=turned[:].rearrange("p (s u) r -> p s r u", u=2))
 
         def y_turn(i):
             y_grouped[i] = work.tile([P, PASSES, P, 2], F32, align_bytes=64, name="y_grouped")
@@ -159,13 +170,13 @@ def tile_block_pb_kernel(tc, attn_out, v, x, wo, attn_scale, out):
                 in_=y_grouped[i][:].rearrange("p s t u -> p (s t u)").bitcast(BF16),
             )
 
-        def wo_turn(half, n):
+        def wo_turn(half, n, copy=nc.scalar.copy):
             if half not in wo_grouped:
                 wo_grouped[half] = weights.tile(
                     [P, PASSES, D_HALF, 2], F32, align_bytes=64, name="wo_grouped"
                 )
             words_to_partitions(
-                wo_rows[half][:, n, :], wo_grouped[half][:, :, n * P : (n + 1) * P, :]
+                wo_rows[half][:, n, :], wo_grouped[half][:, :, n * P : (n + 1) * P, :], copy
             )
 
         def wo_quantise(half):
@@ -216,6 +227,32 @@ def tile_block_pb_kernel(tc, attn_out, v, x, wo, attn_scale, out):
             )
             nc.sync.dma_start(out=out_rows[i][:, cols], in_=result[:])
 
+        def project_tokens(i):
+            token_acc[i] = psum.tile([P, D_HALF], F32, name="bank")
+            for s in range(PASSES):
+                nc.tensor.matmul_mx(
+                    out=token_acc[i][:],
+                    lhsT=y_codes[i][:, s, :].bitcast(FP8X4),
+                    lhsT_scale=y_scales[i][:, s, :],
+                    rhs=wo_codes[0][:, s, :].bitcast(FP8X4),
+                    rhs_scale=wo_scales[0][:, s, :],
+                    start=(s == 0),
+                    stop=(s == PASSES - 1),
+                )
+
+        def scale_tokens(i):
+            token_scaled[i] = work.tile([P, D_HALF], F32, name="token_scaled")
+            nc.vector.tensor_tensor(
+                out=token_scaled[i][:], in0=token_acc[i][:], in1=gain_free[:], op=ALU.mult
+            )
+
+        def finish_tokens(i):
+            result = work.tile([P, D_HALF], F32, name="token_result")
+            nc.gpsimd.tensor_tensor(
+                out=result[:], in0=token_scaled[i][:], in1=x_tiles[i][:, 0:D_HALF], op=ALU.add
+            )
+            nc.sync.dma_start(out=out_rows[i][:, 0:D_HALF], in_=result[:])
+
         ctx.enter_context(tc.manual_schedule())
         squares(0)
         multiply(0)
@@ -225,16 +262,14 @@ def tile_block_pb_kernel(tc, attn_out, v, x, wo, attn_scale, out):
         multiply(1)
         sums(0)
         invert(1)
-        invert(2)
         multiply(2)
         sums(1)
         subtract(0)
         multiply(3)
         squares(3)
         squares(4)
-        invert(3)
-        invert(4)
-        for n in range(D_BLOCKS):
+        invert(2)
+        for n in range(D_BLOCKS - 1):
             wo_turn(0, n)
         gain_turned = psum.tile([P, P], BF16, name="bank")
         nc.tensor.transpose(out=gain_turned[:], in_=gain_rows[:], identity=ident_bf16[:])
@@ -242,6 +277,7 @@ def tile_block_pb_kernel(tc, attn_out, v, x, wo, attn_scale, out):
         nc.scalar.copy(out=gain[:], in_=gain_turned[:, 0 : D // P])
         y_turn(0)
         subtract(1)
+        wo_turn(0, D_BLOCKS - 1, nc.vector.tensor_copy)
         for n in range(D_BLOCKS):
             wo_turn(1, n)
         y_turn(1)
@@ -252,38 +288,46 @@ def tile_block_pb_kernel(tc, attn_out, v, x, wo, attn_scale, out):
         y_quantise(1)
         for i in range(2, T_TILES):
             sums(i)
-        for i in range(2):
-            for half in range(D_HALVES):
-                project(i, half)
+        project(0, 1)
+        project_tokens(0)
+        project(1, 1)
         subtract(2)
         y_turn(2)
+        project_tokens(1)
         subtract(3)
-        y_quantise(2)
         subtract(4)
-        scale(0, 0)
+        y_quantise(2)
         scale(0, 1)
         y_turn(3)
-        project(2, 0)
-        project(2, 1)
-        turn_back(0, 0)
+        y_turn(4)
         turn_back(0, 1)
-        finish(0, 0)
+        project(2, 1)
+        project_tokens(2)
+        scale_tokens(0)
         y_quantise(3)
         finish(0, 1)
-        scale(1, 0)
+        finish_tokens(0)
         scale(1, 1)
-        y_turn(4)
-        turn_back(1, 0)
         turn_back(1, 1)
-        finish(1, 0)
         y_quantise(4)
+        project(3, 1)
+        project_tokens(3)
+        scale_tokens(1)
+        finish_tokens(1)
+        scale_tokens(2)
         finish(1, 1)
-        for i in range(2, T_TILES):
-            for half in range(D_HALVES):
-                scale(i, half)
-            if i + 1 < T_TILES:
-                project(i + 1, 0)
-                project(i + 1, 1)
-            for half in range(D_HALVES):
-                turn_back(i, half)
-                finish(i, half)
+        finish_tokens(2)
+        project(4, 0)
+        project(4, 1)
+        scale(2, 1)
+        turn_back(2, 1)
+        scale_tokens(3)
+        finish(2, 1)
+        finish_tokens(3)
+        scale(3, 1)
+        turn_back(3, 1)
+        finish(3, 1)
+        for half in range(D_HALVES):
+            scale(4, half)
+            turn_back(4, half)
+            finish(4, half)

@@ -20,7 +20,8 @@ C = HKV * G * HD
 D = 1024
 
 T_TILES = T // P
-GROUPS = (1, 2, 2)
+GROUPS = (2, 3)
+A_PARTS = (2, 1)
 PASSES = C // (4 * P)
 D_HALF = 512
 D_HALVES = D // D_HALF
@@ -54,28 +55,35 @@ def tile_block_pb_kernel(tc, attn_out, v, x, wo, attn_scale, out):
             nc.sync.dma_start(
                 out=v_sb[:], in_=v[0, :, rows, :].rearrange("h (p j) d -> p h j d", j=n)
             )
-            a_sb = tokens.tile([P, HKV * G, n, HD], BF16, name="a_sb_%d" % k, bufs=1)
-            nc.sync.dma_start(
-                out=a_sb[:],
-                in_=attn_out[0, :, :, rows, :].rearrange("h g (p j) d -> p (h g) j d", j=n),
-            )
+            parts = []
+            heads = HKV // A_PARTS[k]
+            for part in range(A_PARTS[k]):
+                a_sb = tokens.tile(
+                    [P, heads * G, n, HD], BF16, name="a_sb_%d_%d" % (k, part), bufs=1
+                )
+                nc.sync.dma_start(
+                    out=a_sb[:],
+                    in_=attn_out[0, part * heads : (part + 1) * heads, :, rows, :].rearrange(
+                        "h g (p j) d -> p (h g) j d", j=n
+                    ),
+                )
+                parts.append(a_sb)
             for j in range(n):
                 group_of.append((k, j))
                 v_tiles.append(v_sb[:, :, j, :])
-                a_tiles.append(a_sb[:, :, j, :].rearrange("p (h g) d -> p h g d", g=G))
+                a_tiles.append(
+                    [part[:, :, j, :].rearrange("p (h g) d -> p h g d", g=G) for part in parts]
+                )
                 out_rows.append(out[0, rows, :].rearrange("(p j) d -> p j d", j=n)[:, j, :])
             groups.append((rows, n))
             first += n * P
-            half = k - 1
-            if half in range(D_HALVES):
-                wo_sb = weights.tile([P, D_BLOCKS, C], BF16)
-                nc.sync.dma_start(
-                    out=wo_sb[:],
-                    in_=wo[half * D_HALF : (half + 1) * D_HALF, :].rearrange(
-                        "(n p) c -> p n c", p=P
-                    ),
-                )
-                wo_rows.append(wo_sb)
+        for half in range(D_HALVES):
+            wo_sb = weights.tile([P, D_BLOCKS, C], BF16)
+            nc.sync.dma_start(
+                out=wo_sb[:],
+                in_=wo[half * D_HALF : (half + 1) * D_HALF, :].rearrange("(n p) c -> p n c", p=P),
+            )
+            wo_rows.append(wo_sb)
         for k, (rows, n) in enumerate(groups):
             x_sb = tokens.tile([P, n, D], BF16, name="x_sb_%d" % k, bufs=1)
             nc.sync.dma_start(
@@ -111,11 +119,15 @@ def tile_block_pb_kernel(tc, attn_out, v, x, wo, attn_scale, out):
                     accum_out=v_dot_v[k][:, j, h : h + 1],
                 )
 
-        def multiply(i):
-            products[i] = tokens.tile([P, HKV, G, HD], F32, name="products")
+        def multiply(i, part=0):
+            if i not in products:
+                products[i] = tokens.tile([P, HKV, G, HD], F32, name="products")
+            heads = HKV // len(a_tiles[i])
+            hs = slice(part * heads, (part + 1) * heads)
             nc.vector.tensor_tensor(
-                out=products[i][:], in0=a_tiles[i],
-                in1=v_tiles[i].unsqueeze(2).to_broadcast([P, HKV, G, HD]), op=ALU.mult,
+                out=products[i][:, hs, :, :], in0=a_tiles[i][part],
+                in1=v_tiles[i][:, hs, :].unsqueeze(2).to_broadcast([P, heads, G, HD]),
+                op=ALU.mult,
             )
 
         def invert(k):
@@ -140,11 +152,12 @@ def tile_block_pb_kernel(tc, attn_out, v, x, wo, attn_scale, out):
 
         def subtract(i):
             y_rows[i] = work.tile([P, HKV, G, HD], BF16, align_bytes=64, name="y_rows")
+            heads = HKV // len(a_tiles[i])
             for h in range(HKV):
                 for g in range(G):
                     nc.vector.scalar_tensor_tensor(
                         out=y_rows[i][:, h, g, :], in0=v_tiles[i][:, h, :],
-                        scalar=neg_coef[i][:, h, g : g + 1], in1=a_tiles[i][:, h, g, :],
+                        scalar=neg_coef[i][:, h, g : g + 1], in1=a_tiles[i][h // heads][:, h % heads, g, :],
                         op0=ALU.mult, op1=ALU.add,
                     )
 
@@ -220,7 +233,7 @@ def tile_block_pb_kernel(tc, attn_out, v, x, wo, attn_scale, out):
 
         def finish(i, half):
             cols = slice(half * D_HALF, (half + 1) * D_HALF)
-            result = work.tile([P, D_HALF], F32, name="result", bufs=4)
+            result = work.tile([P, D_HALF], F32, name="result", bufs=6)
             nc.vector.tensor_tensor(
                 out=result[:], in0=back[i, half][:].rearrange("p n d -> p (n d)"),
                 in1=x_tiles[i][:, cols], op=ALU.add,
@@ -247,7 +260,7 @@ def tile_block_pb_kernel(tc, attn_out, v, x, wo, attn_scale, out):
             )
 
         def finish_tokens(i):
-            result = work.tile([P, D_HALF], F32, name="token_result")
+            result = work.tile([P, D_HALF], F32, name="token_result", bufs=4)
             nc.gpsimd.tensor_tensor(
                 out=result[:], in0=token_scaled[i][:], in1=x_tiles[i][:, 0:D_HALF], op=ALU.add
             )
@@ -255,20 +268,22 @@ def tile_block_pb_kernel(tc, attn_out, v, x, wo, attn_scale, out):
 
         ctx.enter_context(tc.manual_schedule())
         squares(0)
-        multiply(0)
-        invert(0)
         squares(1)
-        squares(2)
-        multiply(1)
+        multiply(0, 0)
+        invert(0)
+        multiply(0, 1)
+        multiply(1, 0)
+        multiply(1, 1)
         sums(0)
-        invert(1)
-        multiply(2)
         sums(1)
         subtract(0)
+        multiply(2)
+        subtract(1)
         multiply(3)
-        squares(3)
-        squares(4)
-        invert(2)
+        for i in range(2, T_TILES):
+            squares(i)
+        invert(1)
+        multiply(4)
         for n in range(D_BLOCKS - 1):
             wo_turn(0, n)
         gain_turned = psum.tile([P, P], BF16, name="bank")
@@ -276,26 +291,26 @@ def tile_block_pb_kernel(tc, attn_out, v, x, wo, attn_scale, out):
         gain = const.tile([P, D // P], F32)
         nc.scalar.copy(out=gain[:], in_=gain_turned[:, 0 : D // P])
         y_turn(0)
-        subtract(1)
         wo_turn(0, D_BLOCKS - 1, nc.vector.tensor_copy)
-        for n in range(D_BLOCKS):
+        for n in range(D_BLOCKS - 1):
             wo_turn(1, n)
         y_turn(1)
         y_quantise(0)
         wo_quantise(0)
-        multiply(4)
-        wo_quantise(1)
+        wo_turn(1, D_BLOCKS - 1, nc.vector.tensor_copy)
         y_quantise(1)
+        project_tokens(0)
+        project_tokens(1)
+        wo_quantise(1)
         for i in range(2, T_TILES):
             sums(i)
         project(0, 1)
-        project_tokens(0)
-        project(1, 1)
         subtract(2)
         y_turn(2)
-        project_tokens(1)
+        project(1, 1)
         subtract(3)
         subtract(4)
+        scale_tokens(0)
         y_quantise(2)
         scale(0, 1)
         y_turn(3)
@@ -303,30 +318,29 @@ def tile_block_pb_kernel(tc, attn_out, v, x, wo, attn_scale, out):
         turn_back(0, 1)
         project(2, 1)
         project_tokens(2)
-        scale_tokens(0)
-        y_quantise(3)
-        finish(0, 1)
         finish_tokens(0)
+        scale_tokens(1)
+        y_quantise(3)
+        finish_tokens(1)
+        finish(0, 1)
         scale(1, 1)
         turn_back(1, 1)
         y_quantise(4)
         project(3, 1)
         project_tokens(3)
-        scale_tokens(1)
-        finish_tokens(1)
         scale_tokens(2)
-        finish(1, 1)
         finish_tokens(2)
-        project(4, 0)
-        project(4, 1)
+        finish(1, 1)
         scale(2, 1)
         turn_back(2, 1)
+        project(4, 0)
         scale_tokens(3)
         finish(2, 1)
         finish_tokens(3)
         scale(3, 1)
         turn_back(3, 1)
         finish(3, 1)
+        project(4, 1)
         for half in range(D_HALVES):
             scale(4, half)
             turn_back(4, half)

@@ -20,8 +20,8 @@ C = HKV * G * HD
 D = 1024
 
 T_TILES = T // P
-GROUPS = (2, 3)
-A_PARTS = (2, 1)
+GROUPS = (2, 2, 1)
+A_PARTS = (2, 1, 1)
 PASSES = C // (4 * P)
 D_HALF = 512
 D_HALVES = D // D_HALF
@@ -77,13 +77,16 @@ def tile_block_pb_kernel(tc, attn_out, v, x, wo, attn_scale, out):
                 out_rows.append(out[0, rows, :].rearrange("(p j) d -> p j d", j=n)[:, j, :])
             groups.append((rows, n))
             first += n * P
-        for half in range(D_HALVES):
-            wo_sb = weights.tile([P, D_BLOCKS, C], BF16)
-            nc.sync.dma_start(
-                out=wo_sb[:],
-                in_=wo[half * D_HALF : (half + 1) * D_HALF, :].rearrange("(n p) c -> p n c", p=P),
-            )
-            wo_rows.append(wo_sb)
+            half = k - 1
+            if half in range(D_HALVES):
+                wo_sb = weights.tile([P, D_BLOCKS, C], BF16)
+                nc.sync.dma_start(
+                    out=wo_sb[:],
+                    in_=wo[half * D_HALF : (half + 1) * D_HALF, :].rearrange(
+                        "(n p) c -> p n c", p=P
+                    ),
+                )
+                wo_rows.append(wo_sb)
         for k, (rows, n) in enumerate(groups):
             x_sb = tokens.tile([P, n, D], BF16, name="x_sb_%d" % k, bufs=1)
             nc.sync.dma_start(
@@ -283,6 +286,7 @@ def tile_block_pb_kernel(tc, attn_out, v, x, wo, attn_scale, out):
         for i in range(2, T_TILES):
             squares(i)
         invert(1)
+        invert(2)
         multiply(4)
         for n in range(D_BLOCKS - 1):
             wo_turn(0, n)

@@ -45,6 +45,13 @@ def tile_block_pb_kernel(tc, attn_out, v, x, wo, attn_scale, out):
         groups, group_of, wo_rows = [], [], []
         gain_rows = const.tile([P, P], BF16)
         nc.gpsimd.memset(gain_rows[:], 0.0)
+        gain_row = const.tile([P, D_HALF], BF16)
+        nc.gpsimd.memset(gain_row[:], 0.0)
+        ones = const.tile([P, P], BF16)
+        nc.gpsimd.memset(ones[:], 1.0)
+        nc.scalar.dma_start(
+            out=gain_row[0:1, :], in_=attn_scale[0:D_HALF].rearrange("(o d) -> o d", o=1)
+        )
         nc.scalar.dma_start(
             out=gain_rows[0 : D // P, :], in_=attn_scale.rearrange("(n p) -> n p", p=P)
         )
@@ -95,10 +102,6 @@ def tile_block_pb_kernel(tc, attn_out, v, x, wo, attn_scale, out):
             for j in range(n):
                 x_tiles.append(x_sb[:, j, :])
 
-        gain_free = const.tile([P, D_HALF], BF16)
-        nc.sync.dma_start(
-            out=gain_free[:], in_=attn_scale[0:D_HALF].partition_broadcast(P)
-        )
 
         ident_f32 = const.tile([P, P], F32)
         make_identity(nc, ident_f32[:])
@@ -277,6 +280,12 @@ def tile_block_pb_kernel(tc, attn_out, v, x, wo, attn_scale, out):
         multiply(0, 1)
         multiply(1, 0)
         multiply(1, 1)
+        gain_spread = psum.tile([P, D_HALF], F32, name="bank")
+        nc.tensor.matmul(
+            out=gain_spread[:], lhsT=ones[:], rhs=gain_row[:], start=True, stop=True
+        )
+        gain_free = const.tile([P, D_HALF], BF16)
+        nc.scalar.copy(out=gain_free[:], in_=gain_spread[:])
         sums(0)
         sums(1)
         subtract(0)

@@ -49,12 +49,6 @@ def tile_block_pb_kernel(tc, attn_out, v, x, wo, attn_scale, out):
         nc.gpsimd.memset(gain_row[:], 0.0)
         ones = const.tile([P, P], BF16)
         nc.gpsimd.memset(ones[:], 1.0)
-        nc.scalar.dma_start(
-            out=gain_row[0:1, :], in_=attn_scale[0:D_HALF].rearrange("(o d) -> o d", o=1)
-        )
-        nc.scalar.dma_start(
-            out=gain_rows[0 : D // P, :], in_=attn_scale.rearrange("(n p) -> n p", p=P)
-        )
         first = 0
         for k, n in enumerate(GROUPS):
             rows = slice(first, first + n * P)
@@ -84,6 +78,13 @@ def tile_block_pb_kernel(tc, attn_out, v, x, wo, attn_scale, out):
                 out_rows.append(out[0, rows, :].rearrange("(p j) d -> p j d", j=n)[:, j, :])
             groups.append((rows, n))
             first += n * P
+            if k == 0:
+                nc.sync.dma_start(
+                    out=gain_rows[0 : D // P, :], in_=attn_scale.rearrange("(n p) -> n p", p=P)
+                )
+                nc.sync.dma_start(
+                    out=gain_row[0:1, :], in_=attn_scale[0:D_HALF].rearrange("(o d) -> o d", o=1)
+                )
             half = k - 1
             if half in range(D_HALVES):
                 wo_sb = weights.tile([P, D_BLOCKS, C], BF16)
@@ -280,12 +281,6 @@ def tile_block_pb_kernel(tc, attn_out, v, x, wo, attn_scale, out):
         multiply(0, 1)
         multiply(1, 0)
         multiply(1, 1)
-        gain_spread = psum.tile([P, D_HALF], F32, name="bank")
-        nc.tensor.matmul(
-            out=gain_spread[:], lhsT=ones[:], rhs=gain_row[:], start=True, stop=True
-        )
-        gain_free = const.tile([P, D_HALF], BF16)
-        nc.scalar.copy(out=gain_free[:], in_=gain_spread[:])
         sums(0)
         sums(1)
         subtract(0)
@@ -303,6 +298,12 @@ def tile_block_pb_kernel(tc, attn_out, v, x, wo, attn_scale, out):
         nc.tensor.transpose(out=gain_turned[:], in_=gain_rows[:], identity=ident_bf16[:])
         gain = const.tile([P, D // P], F32)
         nc.scalar.copy(out=gain[:], in_=gain_turned[:, 0 : D // P])
+        gain_spread = psum.tile([P, D_HALF], F32, name="bank")
+        nc.tensor.matmul(
+            out=gain_spread[:], lhsT=ones[:], rhs=gain_row[:], start=True, stop=True
+        )
+        gain_free = const.tile([P, D_HALF], BF16)
+        nc.scalar.copy(out=gain_free[:], in_=gain_spread[:])
         y_turn(0)
         wo_turn(0, D_BLOCKS - 1, nc.vector.tensor_copy)
         for n in range(D_BLOCKS - 1):

@@ -39,7 +39,7 @@ def tile_block_pb_kernel(tc, attn_out, v, x, wo, attn_scale, out):
         weights = ctx.enter_context(tc.tile_pool(name="weights", bufs=D_HALVES))
         tokens = ctx.enter_context(tc.tile_pool(name="tokens", bufs=T_TILES))
         work = ctx.enter_context(tc.tile_pool(name="work", bufs=3))
-        psum = ctx.enter_context(tc.psum_pool(name="psum", bufs=8))
+        psum = ctx.enter_context(tc.psum_pool(name="psum", bufs=5))
 
         a_tiles, v_tiles, x_tiles, out_rows = [], [], [], []
         groups, group_of, wo_rows = [], [], []
@@ -248,7 +248,7 @@ def tile_block_pb_kernel(tc, attn_out, v, x, wo, attn_scale, out):
             nc.sync.dma_start(out=out_rows[i][:, cols], in_=result[:])
 
         def project_tokens(i):
-            token_acc[i] = psum.tile([P, D_HALF], F32, name="bank")
+            token_acc[i] = psum.tile([P, D_HALF], F32, name="token_bank", bufs=3)
             for s in range(PASSES):
                 nc.tensor.matmul_mx(
                     out=token_acc[i][:],
@@ -324,8 +324,8 @@ def tile_block_pb_kernel(tc, attn_out, v, x, wo, attn_scale, out):
         project(1, 1)
         subtract(3)
         subtract(4)
-        scale_tokens(0)
         y_quantise(2)
+        scale_tokens(0)
         scale(0, 1)
         y_turn(3)
         y_turn(4)
@@ -333,27 +333,27 @@ def tile_block_pb_kernel(tc, attn_out, v, x, wo, attn_scale, out):
         project(2, 1)
         project_tokens(2)
         finish_tokens(0)
-        scale_tokens(1)
         y_quantise(3)
-        finish_tokens(1)
         finish(0, 1)
         scale(1, 1)
         turn_back(1, 1)
         y_quantise(4)
         project(3, 1)
         project_tokens(3)
-        scale_tokens(2)
-        finish_tokens(2)
+        scale_tokens(1)
         finish(1, 1)
+        finish_tokens(1)
+        scale_tokens(2)
         scale(2, 1)
         turn_back(2, 1)
         project(4, 0)
         scale_tokens(3)
         finish(2, 1)
-        finish_tokens(3)
+        finish_tokens(2)
         scale(3, 1)
         turn_back(3, 1)
         finish(3, 1)
+        finish_tokens(3)
         project(4, 1)
         for half in range(D_HALVES):
             scale(4, half)

from contextlib import ExitStack

import concourse.mybir as mybir
from concourse.masks import make_identity

F32 = mybir.dt.float32
BF16 = mybir.dt.bfloat16
U32 = mybir.dt.uint32
U8 = mybir.dt.uint8
FP8X4 = mybir.dt.float8_e4m3fn_x4
ALU = mybir.AluOpType
ACT = mybir.ActivationFunctionType

P = 128
T = 640
HKV = 4
G = 2
HD = 128
C = HKV * G * HD
D = 1024

T_TILES = T // P
GROUPS = (2, 2, 1)
A_PARTS = (2, 1, 1)
PASSES = C // (4 * P)
D_HALF = 512
D_HALVES = D // D_HALF
D_BLOCKS = D_HALF // P

EPS_SQUARED = 1e-24

FLOPS = 2 * T * C * D


def tile_block_pb_kernel(tc, attn_out, v, x, wo, attn_scale, out):
    nc = tc.nc
    with ExitStack() as ctx:
        const = ctx.enter_context(tc.tile_pool(name="const", bufs=1))
        weights = ctx.enter_context(tc.tile_pool(name="weights", bufs=D_HALVES))
        tokens = ctx.enter_context(tc.tile_pool(name="tokens", bufs=T_TILES))
        work = ctx.enter_context(tc.tile_pool(name="work", bufs=3))
        psum = ctx.enter_context(tc.psum_pool(name="psum", bufs=5))

        a_tiles, v_tiles, x_tiles, out_rows = [], [], [], []
        groups, group_of, wo_rows = [], [], []
        gain_rows = const.tile([P, P], BF16)
        nc.gpsimd.memset(gain_rows[:], 0.0)
        gain_row = const.tile([P, D_HALF], BF16)
        nc.gpsimd.memset(gain_row[:], 0.0)
        ones = const.tile([P, P], BF16)
        nc.gpsimd.memset(ones[:], 1.0)
        first = 0
        for k, n in enumerate(GROUPS):
            rows = slice(first, first + n * P)
            v_sb = tokens.tile([P, HKV, n, HD], BF16, name="v_sb_%d" % k, bufs=1)
            nc.sync.dma_start(
                out=v_sb[:], in_=v[0, :, rows, :].rearrange("h (p j) d -> p h j d", j=n)
            )
            parts = []
            heads = HKV // A_PARTS[k]
            for part in range(A_PARTS[k]):
                a_sb = tokens.tile(
                    [P, heads * G, n, HD], BF16, name="a_sb_%d_%d" % (k, part), bufs=1
                )
                nc.sync.dma_start(
                    out=a_sb[:],
                    in_=attn_out[0, part * heads : (part + 1) * heads, :, rows, :].rearrange(
                        "h g (p j) d -> p (h g) j d", j=n
                    ),
                )
                parts.append(a_sb)
            for j in range(n):
                group_of.append((k, j))
                v_tiles.append(v_sb[:, :, j, :])
                a_tiles.append(
                    [part[:, :, j, :].rearrange("p (h g) d -> p h g d", g=G) for part in parts]
                )
                out_rows.append(out[0, rows, :].rearrange("(p j) d -> p j d", j=n)[:, j, :])
            groups.append((rows, n))
            first += n * P
            if k == 0:
                nc.sync.dma_start(
                    out=gain_rows[0 : D // P, :], in_=attn_scale.rearrange("(n p) -> n p", p=P)
                )
                nc.sync.dma_start(
                    out=gain_row[0:1, :], in_=attn_scale[0:D_HALF].rearrange("(o d) -> o d", o=1)
                )
            half = k - 1
            if half in range(D_HALVES):
                wo_sb = weights.tile([P, D_BLOCKS, C], BF16)
                nc.sync.dma_start(
                    out=wo_sb[:],
                    in_=wo[half * D_HALF : (half + 1) * D_HALF, :].rearrange(
                        "(n p) c -> p n c", p=P
                    ),
                )
                wo_rows.append(wo_sb)
        for k, (rows, n) in enumerate(groups):
            x_sb = tokens.tile([P, n, D], BF16, name="x_sb_%d" % k, bufs=1)
            nc.sync.dma_start(
                out=x_sb[:], in_=x[0, rows, :].rearrange("(p j) d -> p j d", j=n)
            )
            for j in range(n):
                x_tiles.append(x_sb[:, j, :])


        ident_f32 = const.tile([P, P], F32)
        make_identity(nc, ident_f32[:])
        ident_bf16 = const.tile([P, P], BF16)
        make_identity(nc, ident_bf16[:])

        products, v_dot_v, neg_inv, neg_coef = {}, {}, {}, {}
        y_rows, y_grouped, y_codes, y_scales = {}, {}, {}, {}
        wo_grouped, wo_codes, wo_scales = {}, {}, {}
        acc, scaled, back = {}, {}, {}
        token_acc, token_scaled = {}, {}

        def squares(i):
            k, j = group_of[i]
            if k not in v_dot_v:
                v_dot_v[k] = tokens.tile([P, GROUPS[k], HKV], F32, name="v_dot_v")
            for h in range(HKV):
                scratch = work.tile([P, HD], BF16, name="scratch")
                nc.scalar.activation(
                    out=scratch[:], in_=v_tiles[i][:, h, :], func=ACT.Square,
                    accum_out=v_dot_v[k][:, j, h : h + 1],
                )

        def multiply(i, part=0):
            if i not in products:
                products[i] = tokens.tile([P, HKV, G, HD], F32, name="products")
            heads = HKV // len(a_tiles[i])
            hs = slice(part * heads, (part + 1) * heads)
            nc.vector.tensor_tensor(
                out=products[i][:, hs, :, :], in0=a_tiles[i][part],
                in1=v_tiles[i][:, hs, :].unsqueeze(2).to_broadcast([P, heads, G, HD]),
                op=ALU.mult,
            )

        def invert(k):
            neg_norm = tokens.tile([P, GROUPS[k], HKV], F32, name="neg_norm")
            nc.vector.tensor_scalar(
                out=neg_norm[:], in0=v_dot_v[k][:], scalar1=EPS_SQUARED, scalar2=-1.0,
                op0=ALU.max, op1=ALU.mult,
            )
            neg_inv[k] = tokens.tile([P, GROUPS[k], HKV], F32, name="neg_inv")
            nc.vector.reciprocal(out=neg_inv[k][:], in_=neg_norm[:])

        def sums(i):
            k, j = group_of[i]
            neg_coef[i] = tokens.tile([P, HKV, G], F32, name="neg_coef")
            for h in range(HKV):
                for g in range(G):
                    scratch = work.tile([P, HD], BF16, name="scratch")
                    nc.scalar.activation(
                        out=scratch[:], in_=products[i][:, h, g, :], func=ACT.Copy,
                        scale=neg_inv[k][:, j, h : h + 1], accum_out=neg_coef[i][:, h, g : g + 1],
                    )

        def subtract(i):
            y_rows[i] = work.tile([P, HKV, G, HD], BF16, align_bytes=64, name="y_rows")
            heads = HKV // len(a_tiles[i])
            for h in range(HKV):
                for g in range(G):
                    nc.vector.scalar_tensor_tensor(
                        out=y_rows[i][:, h, g, :], in0=v_tiles[i][:, h, :],
                        scalar=neg_coef[i][:, h, g : g + 1], in1=a_tiles[i][h // heads][:, h % heads, g, :],
                        op0=ALU.mult, op1=ALU.add,
                    )

        def words_to_partitions(rows, grouped, copy=nc.scalar.copy):
            words = rows.bitcast(F32)
            turned = psum.tile([P, PASSES * 2, P], F32, name="bank")
            for j in range(PASSES * 2):
                nc.tensor.transpose(
                    out=turned[:, j, :], in_=words[:, j * P : (j + 1) * P], identity=ident_f32[:]
                )
            copy(out=grouped, in_=turned[:].rearrange("p (s u) r -> p s r u", u=2))

        def y_turn(i):
            y_grouped[i] = work.tile([P, PASSES, P, 2], F32, align_bytes=64, name="y_grouped")
            words_to_partitions(y_rows[i][:].rearrange("p h g d -> p (h g d)"), y_grouped[i][:])

        def y_quantise(i):
            y_codes[i] = tokens.tile([P, PASSES, P], U32, align_bytes=64, name="y_codes")
            y_scales[i] = tokens.tile([P, PASSES, P], U8, align_bytes=64, name="y_scales")
            nc.vector.quantize_mx(
                out=y_codes[i][:].rearrange("p s t -> p (s t)").bitcast(FP8X4),
                scales=y_scales[i][:].rearrange("p s t -> p (s t)"),
                in_=y_grouped[i][:].rearrange("p s t u -> p (s t u)").bitcast(BF16),
            )

        def wo_turn(half, n, copy=nc.scalar.copy):
            if half not in wo_grouped:
                wo_grouped[half] = weights.tile(
                    [P, PASSES, D_HALF, 2], F32, align_bytes=64, name="wo_grouped"
                )
            words_to_partitions(
                wo_rows[half][:, n, :], wo_grouped[half][:, :, n * P : (n + 1) * P, :], copy
            )

        def wo_quantise(half):
            wo_codes[half] = weights.tile([P, PASSES, D_HALF], U32, align_bytes=64, name="wo_codes")
            wo_scales[half] = weights.tile([P, PASSES, D_HALF], U8, align_bytes=64, name="wo_scales")
            nc.vector.quantize_mx(
                out=wo_codes[half][:].rearrange("p s d -> p (s d)").bitcast(FP8X4),
                scales=wo_scales[half][:].rearrange("p s d -> p (s d)"),
                in_=wo_grouped[half][:].rearrange("p s d u -> p (s d u)").bitcast(BF16),
            )

        def project(i, half):
            acc[i, half] = psum.tile([P, D_BLOCKS, P], F32, name="bank")
            for n in range(D_BLOCKS):
                for s in range(PASSES):
                    nc.tensor.matmul_mx(
                        out=acc[i, half][:, n, :],
                        lhsT=wo_codes[half][:, s, n * P : (n + 1) * P].bitcast(FP8X4),
                        lhsT_scale=wo_scales[half][:, s, n * P : (n + 1) * P],
                        rhs=y_codes[i][:, s, :].bitcast(FP8X4),
                        rhs_scale=y_scales[i][:, s, :],
                        start=(s == 0),
                        stop=(s == PASSES - 1),
                    )

        def scale(i, half):
            scaled[i, half] = work.tile([P, D_BLOCKS, P], F32, name="scaled", bufs=4)
            for n in range(D_BLOCKS):
                block = half * D_BLOCKS + n
                nc.scalar.activation(
                    out=scaled[i, half][:, n, :], in_=acc[i, half][:, n, :], func=ACT.Copy,
                    scale=gain[:, block : block + 1],
                )

        def turn_back(i, half):
            back[i, half] = psum.tile([P, D_BLOCKS, P], F32, name="bank")
            for n in range(D_BLOCKS):
                nc.tensor.transpose(
                    out=back[i, half][:, n, :], in_=scaled[i, half][:, n, :], identity=ident_f32[:]
                )

        def finish(i, half):
            cols = slice(half * D_HALF, (half + 1) * D_HALF)
            result = work.tile([P, D_HALF], F32, name="result", bufs=6)
            nc.vector.tensor_tensor(
                out=result[:], in0=back[i, half][:].rearrange("p n d -> p (n d)"),
                in1=x_tiles[i][:, cols], op=ALU.add,
            )
            nc.sync.dma_start(out=out_rows[i][:, cols], in_=result[:])

        def project_tokens(i):
            token_acc[i] = psum.tile([P, D_HALF], F32, name="token_bank", bufs=3)
            for s in range(PASSES):
                nc.tensor.matmul_mx(
                    out=token_acc[i][:],
                    lhsT=y_codes[i][:, s, :].bitcast(FP8X4),
                    lhsT_scale=y_scales[i][:, s, :],
                    rhs=wo_codes[0][:, s, :].bitcast(FP8X4),
                    rhs_scale=wo_scales[0][:, s, :],
                    start=(s == 0),
                    stop=(s == PASSES - 1),
                )

        def scale_tokens(i):
            token_scaled[i] = work.tile([P, D_HALF], F32, name="token_scaled")
            nc.vector.tensor_tensor(
                out=token_scaled[i][:], in0=token_acc[i][:], in1=gain_free[:], op=ALU.mult
            )

        def finish_tokens(i):
            result = work.tile([P, D_HALF], F32, name="token_result", bufs=4)
            nc.gpsimd.tensor_tensor(
                out=result[:], in0=token_scaled[i][:], in1=x_tiles[i][:, 0:D_HALF], op=ALU.add
            )
            nc.sync.dma_start(out=out_rows[i][:, 0:D_HALF], in_=result[:])

        ctx.enter_context(tc.manual_schedule())
        squares(0)
        squares(1)
        multiply(0, 0)
        invert(0)
        multiply(0, 1)
        multiply(1, 0)
        multiply(1, 1)
        sums(0)
        sums(1)
        subtract(0)
        multiply(2)
        subtract(1)
        multiply(3)
        for i in range(2, T_TILES):
            squares(i)
        invert(1)
        invert(2)
        multiply(4)
        for n in range(D_BLOCKS - 1):
            wo_turn(0, n)
        gain_turned = psum.tile([P, P], BF16, name="bank")
        nc.tensor.transpose(out=gain_turned[:], in_=gain_rows[:], identity=ident_bf16[:])
        gain = const.tile([P, D // P], F32)
        nc.scalar.copy(out=gain[:], in_=gain_turned[:, 0 : D // P])
        gain_spread = psum.tile([P, D_HALF], F32, name="bank")
        nc.tensor.matmul(
            out=gain_spread[:], lhsT=ones[:], rhs=gain_row[:], start=True, stop=True
        )
        gain_free = const.tile([P, D_HALF], BF16)
        nc.scalar.copy(out=gain_free[:], in_=gain_spread[:])
        y_turn(0)
        wo_turn(0, D_BLOCKS - 1, nc.vector.tensor_copy)
        for n in range(D_BLOCKS - 1):
            wo_turn(1, n)
        y_turn(1)
        y_quantise(0)
        wo_quantise(0)
        wo_turn(1, D_BLOCKS - 1, nc.vector.tensor_copy)
        y_quantise(1)
        project_tokens(0)
        project_tokens(1)
        wo_quantise(1)
        for i in range(2, T_TILES):
            sums(i)
        project(0, 1)
        subtract(2)
        y_turn(2)
        project(1, 1)
        subtract(3)
        subtract(4)
        y_quantise(2)
        scale_tokens(0)
        scale(0, 1)
        y_turn(3)
        y_turn(4)
        turn_back(0, 1)
        project(2, 1)
        project_tokens(2)
        finish_tokens(0)
        y_quantise(3)
        finish(0, 1)
        scale(1, 1)
        turn_back(1, 1)
        y_quantise(4)
        project(3, 1)
        project_tokens(3)
        scale_tokens(1)
        finish(1, 1)
        finish_tokens(1)
        scale_tokens(2)
        scale(2, 1)
        turn_back(2, 1)
        project(4, 0)
        scale_tokens(3)
        finish(2, 1)
        finish_tokens(2)
        scale(3, 1)
        turn_back(3, 1)
        finish(3, 1)
        finish_tokens(3)
        project(4, 1)
        for half in range(D_HALVES):
            scale(4, half)
            turn_back(4, half)
            finish(4, half)
